import numpy as np
import ml_dtypes


def mxq(x, axis, fmt="e4m3"):
    dtype, down = {"e4m3": (ml_dtypes.float8_e4m3fn, 7), "e5m2": (ml_dtypes.float8_e5m2, 14)}[fmt]
    v = np.moveaxis(np.asarray(x, np.float32).astype(ml_dtypes.bfloat16).astype(np.float64), axis, -1)
    blocks = v.reshape(v.shape[:-1] + (-1, 32))
    amax = np.abs(blocks).max(-1, keepdims=True)
    byte = np.maximum(np.where(amax > 0, np.frexp(amax)[1] - 1 + 127, 0) - down, 1)
    scale = np.exp2(byte - 127.0)
    codes = (blocks / scale).astype(np.float32).astype(dtype).astype(np.float64)
    return np.moveaxis((codes * scale).reshape(v.shape), -1, axis)


WIDE = False


def mx_kscale(k):
    if not WIDE:
        return np.ones(k)
    levels = np.array([10, -10, 5, -5, 0])
    a = np.random.permutation(np.resize(levels, k // 512 * 4)).reshape(k // 512, 4)
    idx = np.arange(k)
    return np.exp2(a[idx // 512, idx % 128 // 32])


BF16 = ml_dtypes.bfloat16


def bf(x):
    return np.asarray(x, np.float32).astype(BF16)


def f64(x):
    return np.asarray(x).astype(np.float64)


B, H, W, C, NF, ZD = 128, 4, 4, 512, 512, 512
EPS = 1e-8
LRELU_SLOPE = 0.2


def setup_inputs():
    s = mx_kscale(C)
    return {"x": bf(np.random.standard_normal((B, H, W, C)) * s),
            "dlatents": bf(np.random.standard_normal((B, ZD))),
            "noise_map": bf(np.random.standard_normal((B, H, W, 1))),
            "conv_w": bf(np.random.standard_normal((C, NF)) / np.sqrt(C) / s[:, None]),
            "noise_weight": bf(np.random.standard_normal((1, 1, 1, NF)) * 0.5),
            "bias": bf(np.random.standard_normal((1, 1, 1, NF)) * 0.5),
            "dense_w": bf(np.random.standard_normal((ZD, 2 * NF)) / np.sqrt(ZD)),
            "dense_b": bf(np.random.standard_normal(2 * NF) * 0.3)}


def reference(x, dlatents, noise_map, conv_w, noise_weight, bias, dense_w, dense_b):
    y = mxq(f64(x), 3, "e4m3") @ mxq(f64(conv_w), 0, "e4m3")
    y = y + f64(noise_weight) * f64(noise_map) + f64(bias)
    y = np.where(y >= 0.0, y, LRELU_SLOPE * y)
    mu = np.mean(y, axis=(1, 2), keepdims=True)
    var = np.mean(np.square(y - mu), axis=(1, 2), keepdims=True)
    yn = (y - mu) / np.sqrt(var + EPS)
    gb = f64(dlatents) @ f64(dense_w) + f64(dense_b)
    nf = y.shape[-1]
    gb = gb.reshape(-1, 2, 1, 1, nf)
    gamma, beta = gb[:, 0], gb[:, 1]
    return yn * (1.0 + gamma) + beta

@@ -1,0 +1,267 @@
+from contextlib import ExitStack
+
+import concourse.mybir as mybir
+from concourse.masks import make_identity
+
+FLOPS = 2 * 2048 * 512 * 512 + 2 * 128 * 512 * 1024
+
+F32 = mybir.dt.float32
+BF16 = mybir.dt.bfloat16
+U32 = mybir.dt.uint32
+U8 = mybir.dt.uint8
+FP8X4 = mybir.dt.float8_e4m3fn_x4
+ALU = mybir.AluOpType
+ACT = mybir.ActivationFunctionType
+
+P = 128
+HW = 16
+NG = 4
+NCT = 4
+EPS = 1e-8
+SLOPE = 0.2
+
+
+def tile_styleganlayerepilogue_kernel(
+    tc, x, dlatents, noise_map, conv_w, noise_weight, bias, dense_w, dense_b, out
+):
+    nc = tc.nc
+    with ExitStack() as ctx:
+        keep = ctx.enter_context(tc.tile_pool(name="keep", bufs=1))
+        work = ctx.enter_context(tc.tile_pool(name="work", bufs=3))
+        small = ctx.enter_context(tc.tile_pool(name="small", bufs=2))
+        ps = ctx.enter_context(tc.psum_pool(name="ps", bufs=2))
+
+        ident_f = keep.tile([P, P], F32, name="ident_f")
+        make_identity(nc, ident_f[:])
+        ident_b = keep.tile([P, P], BF16, name="ident_b")
+        make_identity(nc, ident_b[:])
+        rows = keep.tile([P, P], BF16, name="rows")
+        nc.gpsimd.memset(rows[:], 0.0)
+        warm = keep.tile([P, 1], F32, name="warm")
+        nc.vector.memset(warm[:], 1.0)
+        warm2 = keep.tile([P, 1], F32, name="warm2")
+        nc.scalar.sqrt(out=warm2[:], in_=warm[:])
+
+        xv = x.rearrange("b h w c -> b (h w c)")
+        x_sb = [keep.tile([P, 2048], BF16, name="x_sb%d" % g) for g in range(NG)]
+        w_raw = keep.tile([P, 4, 512], BF16, name="w_raw")
+        nm_sb = keep.tile([P, HW], BF16, name="nm_sb")
+        dl_sb = keep.tile([P, 512], BF16, name="dl_sb")
+        dw_sb = keep.tile([P, 4, 1024], BF16, name="dw_sb")
+
+        nc.scalar.dma_start(out=nm_sb[:], in_=noise_map.rearrange("b h w o -> b (h w o)"))
+        nc.scalar.dma_start(
+            out=rows[0:4, :], in_=noise_weight.rearrange("a b c (r n) -> (a b c r) n", r=4)
+        )
+        nc.scalar.dma_start(out=rows[4:8, :], in_=bias.rearrange("a b c (r n) -> (a b c r) n", r=4))
+        nc.scalar.dma_start(out=rows[8:16, :], in_=dense_b.rearrange("(r n) -> r n", r=8))
+        nc.sync.dma_start(out=x_sb[0][:], in_=xv[:, 0:2048])
+        nc.sync.dma_start(
+            out=w_raw[:].rearrange("p (u e) c -> p u (e c)", u=2),
+            in_=conv_w.rearrange("(u q e) c -> q u (e c)", u=2, e=2),
+        )
+        for g in range(1, NG):
+            nc.sync.dma_start(out=x_sb[g][:], in_=xv[:, g * 2048 : (g + 1) * 2048])
+        nc.sync.dma_start(out=dl_sb[:], in_=dlatents)
+        nc.sync.dma_start(out=dw_sb[:], in_=dense_w.rearrange("(k p) n -> p k n", p=P))
+
+        cols_ps = ps.tile([P, P], BF16, name="cols_ps", tag="f")
+        nc.tensor.transpose(cols_ps[:], rows[:], ident_b[:])
+        cols = keep.tile([P, 16], F32, name="cols")
+        nc.vector.tensor_copy(out=cols[:], in_=cols_ps[:, 0:16])
+        g1b = keep.tile([P, 4], F32, name="g1b")
+        nc.vector.tensor_scalar_add(out=g1b[:], in0=cols[:, 8:12], scalar1=1.0)
+
+        nm_bc = keep.tile([P, 2048], BF16, name="nm_bc")
+        for half in range(2):
+            nm_ps = ps.tile([P, 1024], BF16, name="nm_ps", tag="s")
+            for j in range(8):
+                hw = half * 8 + j
+                nc.tensor.matmul(
+                    out=nm_ps[:, j * P : (j + 1) * P],
+                    lhsT=nm_sb[:, hw : hw + 1].to_broadcast([P, P]),
+                    rhs=ident_b[:],
+                    start=True,
+                    stop=True,
+                )
+            nc.scalar.copy(out=nm_bc[:, half * 1024 : (half + 1) * 1024], in_=nm_ps[:])
+
+        t_add = [keep.tile([P, 2048], F32, name="t_add%d" % ct) for ct in range(NCT)]
+        for ct in range(NCT):
+            nc.gpsimd.tensor_scalar(
+                out=t_add[ct][:],
+                in0=nm_bc[:],
+                scalar1=cols[:, ct : ct + 1],
+                scalar2=cols[:, 4 + ct : 5 + ct],
+                op0=ALU.mult,
+                op1=ALU.add,
+            )
+
+        w_grp = keep.tile([P, 512, 4], BF16, name="w_grp", align_bytes=64)
+        w_codes = keep.tile([P, 512], U32, name="w_codes", align_bytes=64)
+        w_scales = keep.tile([P, 512], U8, name="w_scales", align_bytes=64)
+        nc.vector.tensor_copy(out=w_grp[:], in_=w_raw[:].rearrange("p t c -> p c t"))
+        nc.vector.quantize_mx(
+            out=w_codes[:].bitcast(FP8X4),
+            scales=w_scales[:],
+            in_=w_grp[:].rearrange("p c t -> p (c t)"),
+        )
+
+        x_grp = [keep.tile([P, 2048], BF16, name="x_grp%d" % g, align_bytes=64) for g in range(NG)]
+        x_codes = [keep.tile([P, 512], U32, name="x_codes%d" % g, align_bytes=64) for g in range(NG)]
+        x_scales = [keep.tile([P, 512], U8, name="x_scales%d" % g, align_bytes=64) for g in range(NG)]
+        for g in range(NG):
+            xw = x_sb[g][:].bitcast(F32)
+            xgw = x_grp[g][:].bitcast(F32)
+            for hh in range(2):
+                xt = ps.tile([P, 4, P], F32, name="xt", tag="o")
+                for j in range(4):
+                    col = (hh * 2 + j // 2) * 256 + (j % 2) * P
+                    nc.tensor.transpose(xt[:, j, :], xw[:, col : col + P], ident_f[:])
+                nc.scalar.copy(
+                    out=xgw[:, hh * 512 : (hh + 1) * 512].rearrange(
+                        "p (h b u) -> p h b u", h=2, u=2
+                    ),
+                    in_=xt[:].rearrange("p (h u) b -> p h b u", h=2),
+                )
+            nc.vector.quantize_mx(
+                out=x_codes[g][:].bitcast(FP8X4), scales=x_scales[g][:], in_=x_grp[g][:]
+            )
+
+        dlT_ps = ps.tile([P, 4, P], BF16, name="dlT_ps", tag="f")
+        for kc in range(4):
+            nc.tensor.transpose(dlT_ps[:, kc, :], dl_sb[:, kc * P : (kc + 1) * P], ident_b[:])
+        dlT = keep.tile([P, 4, P], BF16, name="dlT")
+        nc.vector.tensor_copy(out=dlT[:], in_=dlT_ps[:])
+        gb_sb = [keep.tile([P, 4, P], F32, name="gb_sb%d" % h) for h in range(2)]
+        for half in range(2):
+            gb_ps = ps.tile([P, 4, P], F32, name="gb_ps", tag="f")
+            for ct in range(NCT):
+                nt = half * 4 + ct
+                for kc in range(4):
+                    nc.tensor.matmul(
+                        out=gb_ps[:, ct, :],
+                        lhsT=dw_sb[:, kc, nt * P : (nt + 1) * P],
+                        rhs=dlT[:, kc, :],
+                        start=(kc == 0),
+                        stop=(kc == 3),
+                    )
+            for ct in range(NCT):
+                col = g1b[:, ct : ct + 1] if half == 0 else cols[:, 12 + ct : 13 + ct]
+                nc.scalar.activation(
+                    out=gb_sb[half][:, ct, :], in_=gb_ps[:, ct, :], func=ACT.Identity, bias=col, scale=1.0
+                )
+
+        outv = out.rearrange("b h w c -> b (h w) c")
+        y_sb = {}
+        scale_t = {}
+        shift_t = {}
+
+        def phase1(ct):
+            sums = ps.tile([P, 2, P], F32, name="sums", tag="s")
+            sq = []
+            for g in range(NG):
+                acc = ps.tile([P, 512], F32, name="acc", tag="p")
+                nc.tensor.matmul_mx(
+                    out=acc[:],
+                    lhsT=w_codes[:, ct * P : (ct + 1) * P].bitcast(FP8X4),
+                    lhsT_scale=w_scales[:, ct * P : (ct + 1) * P],
+                    rhs=x_codes[g][:].bitcast(FP8X4),
+                    rhs_scale=x_scales[g][:],
+                    start=True,
+                    stop=True,
+                )
+                z = work.tile([P, 512], F32, name="z", tag="z")
+                nc.vector.tensor_tensor(
+                    out=z[:], in0=acc[:], in1=t_add[ct][:, g * 512 : (g + 1) * 512], op=ALU.add
+                )
+                yt = keep.tile([P, 512], F32, name="y%d_%d" % (ct, g))
+                nc.vector.scalar_tensor_tensor(
+                    out=yt[:], in0=z[:], scalar=SLOPE, in1=z[:], op0=ALU.mult, op1=ALU.max
+                )
+                y_sb[(ct, g)] = yt
+                qt = work.tile([P, 512], F32, name="qt", tag="q", bufs=8)
+                nc.scalar.activation(out=qt[:], in_=yt[:], func=ACT.Square)
+                sq.append(qt)
+                for j in range(4):
+                    hw = g * 4 + j
+                    nc.tensor.matmul(
+                        out=sums[:, 0, :],
+                        lhsT=yt[:, j * P : (j + 1) * P],
+                        rhs=ident_f[:],
+                        is_transpose=True,
+                        start=(hw == 0),
+                        stop=(hw == HW - 1),
+                    )
+            for g in range(NG):
+                for j in range(4):
+                    hw = g * 4 + j
+                    nc.tensor.matmul(
+                        out=sums[:, 1, :],
+                        lhsT=sq[g][:, j * P : (j + 1) * P],
+                        rhs=ident_f[:],
+                        is_transpose=True,
+                        start=(hw == 0),
+                        stop=(hw == HW - 1),
+                    )
+            sc = small.tile([P, 2, P], F32, name="sc", tag="sc")
+            nc.scalar.activation(out=sc[:], in_=sums[:], func=ACT.Copy, scale=1.0 / HW)
+            st = ps.tile([P, 2, P], F32, name="st", tag="f")
+            nc.tensor.transpose(st[:, 0, :], sc[:, 0, :], ident_f[:])
+            nc.tensor.transpose(st[:, 1, :], sc[:, 1, :], ident_f[:])
+            msq = small.tile([P, P], F32, name="msq", tag="msq")
+            nc.scalar.activation(out=msq[:], in_=st[:, 0, :], func=ACT.Square)
+            var = small.tile([P, P], F32, name="var", tag="var")
+            nc.vector.tensor_tensor(out=var[:], in0=st[:, 1, :], in1=msq[:], op=ALU.subtract)
+            var2 = small.tile([P, P], F32, name="var2", tag="var2")
+            nc.vector.tensor_scalar(
+                out=var2[:], in0=var[:], scalar1=0.0, scalar2=EPS, op0=ALU.max, op1=ALU.add
+            )
+            sd = small.tile([P, P], F32, name="sd", tag="sd")
+            nc.scalar.sqrt(out=sd[:], in_=var2[:])
+            rstd = small.tile([P, P], F32, name="rstd", tag="rstd")
+            nc.vector.reciprocal(out=rstd[:], in_=sd[:])
+            a_t = small.tile([P, P], F32, name="a_t", tag="a_t")
+            nc.vector.tensor_tensor(out=a_t[:], in0=rstd[:], in1=gb_sb[0][:, ct, :], op=ALU.mult)
+            m_a = small.tile([P, P], F32, name="m_a", tag="m_a")
+            nc.vector.tensor_tensor(out=m_a[:], in0=st[:, 0, :], in1=a_t[:], op=ALU.mult)
+            b_t = small.tile([P, P], F32, name="b_t", tag="b_t")
+            nc.vector.tensor_tensor(out=b_t[:], in0=gb_sb[1][:, ct, :], in1=m_a[:], op=ALU.subtract)
+            scale_t[ct] = a_t
+            shift_t[ct] = b_t
+
+        def phase2(ct):
+            a_t = scale_t[ct]
+            b_t = shift_t[ct]
+            for g in range(NG):
+                wt = work.tile([P, 4, P], F32, name="wt", tag="w")
+                nc.vector.tensor_tensor(
+                    out=wt[:],
+                    in0=y_sb[(ct, g)][:].rearrange("p (h b) -> p h b", h=4),
+                    in1=a_t[:].unsqueeze(1).to_broadcast([P, 4, P]),
+                    op=ALU.mult,
+                )
+                o_ps = ps.tile([P, 4, P], F32, name="o_ps", tag="o")
+                for j in range(4):
+                    nc.tensor.matmul(
+                        out=o_ps[:, j, :], lhsT=b_t[:], rhs=ident_f[:], is_transpose=True,
+                        start=True, stop=False,
+                    )
+                    nc.tensor.matmul(
+                        out=o_ps[:, j, :], lhsT=wt[:, j, :], rhs=ident_f[:], is_transpose=True,
+                        start=False, stop=True,
+                    )
+                ot = work.tile([P, 4, P], F32, name="ot", tag="ot", bufs=4)
+                nc.scalar.copy(out=ot[:], in_=o_ps[:])
+                nc.sync.dma_start(
+                    out=outv[:, g * 4 : (g + 1) * 4, ct * P : (ct + 1) * P], in_=ot[:]
+                )
+
+        phase1(0)
+        phase1(1)
+        phase2(0)
+        phase1(2)
+        phase2(1)
+        phase1(3)
+        phase2(2)
+        phase2(3)

@@ -17,8 +17,11 @@ P = 128
 HW = 16
 NG = 4
 NCT = 4
+NSTEP = NG * NCT
 EPS = 1e-8
 SLOPE = 0.2
+LAG = 8
+EXTRA_MX = 0
 
 
 def tile_styleganlayerepilogue_kernel(
@@ -29,18 +32,18 @@ def tile_styleganlayerepilogue_kernel(
         keep = ctx.enter_context(tc.tile_pool(name="keep", bufs=1))
         work = ctx.enter_context(tc.tile_pool(name="work", bufs=3))
         small = ctx.enter_context(tc.tile_pool(name="small", bufs=2))
-        ps = ctx.enter_context(tc.psum_pool(name="ps", bufs=2))
+        ps = ctx.enter_context(tc.psum_pool(name="ps", bufs=1))
+        ctx.enter_context(tc.manual_schedule())
 
-        ident_f = keep.tile([P, P], F32, name="ident_f")
-        make_identity(nc, ident_f[:])
-        ident_b = keep.tile([P, P], BF16, name="ident_b")
-        make_identity(nc, ident_b[:])
         rows = keep.tile([P, P], BF16, name="rows")
         nc.gpsimd.memset(rows[:], 0.0)
+        ident_b = keep.tile([P, P], BF16, name="ident_b")
+        make_identity(nc, ident_b[:])
+        ident_f = keep.tile([P, P], F32, name="ident_f")
+        make_identity(nc, ident_f[:])
         warm = keep.tile([P, 1], F32, name="warm")
         nc.vector.memset(warm[:], 1.0)
         warm2 = keep.tile([P, 1], F32, name="warm2")
-        nc.scalar.sqrt(out=warm2[:], in_=warm[:])
 
         xv = x.rearrange("b h w c -> b (h w c)")
         x_sb = [keep.tile([P, 2048], BF16, name="x_sb%d" % g) for g in range(NG)]
@@ -55,12 +58,12 @@ def tile_styleganlayerepilogue_kernel(
         )
         nc.scalar.dma_start(out=rows[4:8, :], in_=bias.rearrange("a b c (r n) -> (a b c r) n", r=4))
         nc.scalar.dma_start(out=rows[8:16, :], in_=dense_b.rearrange("(r n) -> r n", r=8))
-        nc.sync.dma_start(out=x_sb[0][:], in_=xv[:, 0:2048])
+        nc.scalar.sqrt(out=warm2[:], in_=warm[:])
         nc.sync.dma_start(
             out=w_raw[:].rearrange("p (u e) c -> p u (e c)", u=2),
             in_=conv_w.rearrange("(u q e) c -> q u (e c)", u=2, e=2),
         )
-        for g in range(1, NG):
+        for g in range(NG):
             nc.sync.dma_start(out=x_sb[g][:], in_=xv[:, g * 2048 : (g + 1) * 2048])
         nc.sync.dma_start(out=dl_sb[:], in_=dlatents)
         nc.sync.dma_start(out=dw_sb[:], in_=dense_w.rearrange("(k p) n -> p k n", p=P))
@@ -72,9 +75,9 @@ def tile_styleganlayerepilogue_kernel(
         g1b = keep.tile([P, 4], F32, name="g1b")
         nc.vector.tensor_scalar_add(out=g1b[:], in0=cols[:, 8:12], scalar1=1.0)
 
-        nm_bc = keep.tile([P, 2048], BF16, name="nm_bc")
+        nm_bc = [keep.tile([P, 1024], BF16, name="nm_bc%d" % h) for h in range(2)]
         for half in range(2):
-            nm_ps = ps.tile([P, 1024], BF16, name="nm_ps", tag="s")
+            nm_ps = ps.tile([P, 1024], BF16, name="nm_ps%d" % half, tag=("sy" if half == 0 else "sq"))
             for j in range(8):
                 hw = half * 8 + j
                 nc.tensor.matmul(
@@ -84,13 +87,15 @@ def tile_styleganlayerepilogue_kernel(
                     start=True,
                     stop=True,
                 )
-            nc.scalar.copy(out=nm_bc[:, half * 1024 : (half + 1) * 1024], in_=nm_ps[:])
+            nc.scalar.copy(out=nm_bc[half][:], in_=nm_ps[:])
 
-        t_add = [keep.tile([P, 2048], F32, name="t_add%d" % ct) for ct in range(NCT)]
-        for ct in range(NCT):
+        t_add = {}
+        for s in range(NSTEP):
+            ct, g = s // NG, s % NG
+            t_add[s] = keep.tile([P, 512], F32, name="t_add%d" % s)
             nc.gpsimd.tensor_scalar(
-                out=t_add[ct][:],
-                in0=nm_bc[:],
+                out=t_add[s][:],
+                in0=nm_bc[g // 2][:, (g % 2) * 512 : (g % 2 + 1) * 512],
                 scalar1=cols[:, ct : ct + 1],
                 scalar2=cols[:, 4 + ct : 5 + ct],
                 op0=ALU.mult,
@@ -110,11 +115,22 @@ def tile_styleganlayerepilogue_kernel(
         x_grp = [keep.tile([P, 2048], BF16, name="x_grp%d" % g, align_bytes=64) for g in range(NG)]
         x_codes = [keep.tile([P, 512], U32, name="x_codes%d" % g, align_bytes=64) for g in range(NG)]
         x_scales = [keep.tile([P, 512], U8, name="x_scales%d" % g, align_bytes=64) for g in range(NG)]
-        for g in range(NG):
+        outv = out.rearrange("b h w c -> b (h w) c")
+        acc_t = {}
+        y_t = {}
+        q_t = {}
+        w_t = {}
+        sum_t = {}
+        st_t = {}
+        sm = {}
+        gb_sb = [keep.tile([P, 4, P], F32, name="gb_sb%d" % h) for h in range(2)]
+        dlT = keep.tile([P, 4, P], BF16, name="dlT")
+
+        def x_turn(g):
             xw = x_sb[g][:].bitcast(F32)
             xgw = x_grp[g][:].bitcast(F32)
             for hh in range(2):
-                xt = ps.tile([P, 4, P], F32, name="xt", tag="o")
+                xt = ps.tile([P, 4, P], F32, name="xt", tag="o", bufs=2)
                 for j in range(4):
                     col = (hh * 2 + j // 2) * 256 + (j % 2) * P
                     nc.tensor.transpose(xt[:, j, :], xw[:, col : col + P], ident_f[:])
@@ -124,18 +140,142 @@ def tile_styleganlayerepilogue_kernel(
                     ),
                     in_=xt[:].rearrange("p (h u) b -> p h b u", h=2),
                 )
+
+        def x_quant(g):
             nc.vector.quantize_mx(
                 out=x_codes[g][:].bitcast(FP8X4), scales=x_scales[g][:], in_=x_grp[g][:]
             )
 
-        dlT_ps = ps.tile([P, 4, P], BF16, name="dlT_ps", tag="f")
-        for kc in range(4):
-            nc.tensor.transpose(dlT_ps[:, kc, :], dl_sb[:, kc * P : (kc + 1) * P], ident_b[:])
-        dlT = keep.tile([P, 4, P], BF16, name="dlT")
-        nc.vector.tensor_copy(out=dlT[:], in_=dlT_ps[:])
-        gb_sb = [keep.tile([P, 4, P], F32, name="gb_sb%d" % h) for h in range(2)]
-        for half in range(2):
-            gb_ps = ps.tile([P, 4, P], F32, name="gb_ps", tag="f")
+        def mx(s, times=1):
+            ct, g = s // NG, s % NG
+            acc = ps.tile([P, 512], F32, name="acc", tag="p", bufs=3)
+            for rep in range(times):
+                nc.tensor.matmul_mx(
+                    out=acc[:],
+                    lhsT=w_codes[:, ct * P : (ct + 1) * P].bitcast(FP8X4),
+                    lhsT_scale=w_scales[:, ct * P : (ct + 1) * P],
+                    rhs=x_codes[g][:].bitcast(FP8X4),
+                    rhs_scale=x_scales[g][:],
+                    start=True,
+                    stop=True,
+                )
+            acc_t[s] = acc
+
+        def zy(s):
+            z = work.tile([P, 512], F32, name="z", tag="z")
+            nc.vector.tensor_tensor(out=z[:], in0=acc_t[s][:], in1=t_add[s][:], op=ALU.add)
+            yt = keep.tile([P, 512], F32, name="y%d" % s)
+            nc.vector.scalar_tensor_tensor(
+                out=yt[:], in0=z[:], scalar=SLOPE, in1=z[:], op0=ALU.mult, op1=ALU.max
+            )
+            y_t[s] = yt
+
+        def square(s):
+            qt = work.tile([P, 512], F32, name="qt", tag="q")
+            nc.scalar.activation(out=qt[:], in_=y_t[s][:], func=ACT.Square)
+            q_t[s] = qt
+
+        def sums(s):
+            ct, g = s // NG, s % NG
+            if g == 0:
+                sum_y = ps.tile([P, P], F32, name="sum_y", tag="sy")
+                sum_q = ps.tile([P, P], F32, name="sum_q", tag="sq")
+                sum_t[ct] = (sum_y, sum_q)
+            for k in range(2):
+                src = y_t[s] if k == 0 else q_t[s]
+                for j in range(4):
+                    hw = g * 4 + j
+                    nc.tensor.matmul(
+                        out=sum_t[ct][k][:],
+                        lhsT=src[:, j * P : (j + 1) * P],
+                        rhs=ident_f[:],
+                        is_transpose=True,
+                        start=(hw == 0),
+                        stop=(hw == HW - 1),
+                    )
+
+        def stats_scale(ct):
+            sc = small.tile([P, 2, P], F32, name="sc", tag="sc")
+            for k in range(2):
+                nc.scalar.activation(
+                    out=sc[:, k, :], in_=sum_t[ct][k][:], func=ACT.Copy, scale=1.0 / HW
+                )
+            sm[("sc", ct)] = sc
+
+        def stats_turn(ct):
+            st = ps.tile([P, 2, P], F32, name="st", tag="f")
+            for k in range(2):
+                nc.tensor.transpose(st[:, k, :], sm[("sc", ct)][:, k, :], ident_f[:])
+            st_t[ct] = st
+
+        def stats_a(ct):
+            msq = small.tile([P, P], F32, name="msq", tag="msq")
+            nc.scalar.activation(out=msq[:], in_=st_t[ct][:, 0, :], func=ACT.Square)
+            mean = small.tile([P, P], F32, name="mean", tag="mean")
+            nc.scalar.copy(out=mean[:], in_=st_t[ct][:, 0, :])
+            sm[("msq", ct)] = msq
+            sm[("mean", ct)] = mean
+
+        def stats_b(ct):
+            var = small.tile([P, P], F32, name="var", tag="var")
+            nc.vector.tensor_tensor(
+                out=var[:], in0=st_t[ct][:, 1, :], in1=sm[("msq", ct)][:], op=ALU.subtract
+            )
+            var2 = small.tile([P, P], F32, name="var2", tag="var2")
+            nc.vector.tensor_scalar(
+                out=var2[:], in0=var[:], scalar1=0.0, scalar2=EPS, op0=ALU.max, op1=ALU.add
+            )
+            sd = small.tile([P, P], F32, name="sd", tag="sd")
+            nc.scalar.sqrt(out=sd[:], in_=var2[:])
+            sm[("sd", ct)] = sd
+
+        def stats_c(ct):
+            rstd = small.tile([P, P], F32, name="rstd", tag="rstd")
+            nc.vector.reciprocal(out=rstd[:], in_=sm[("sd", ct)][:])
+            a_t = small.tile([P, P], F32, name="a_t", tag="a_t", bufs=3)
+            nc.vector.tensor_tensor(out=a_t[:], in0=rstd[:], in1=gb_sb[0][:, ct, :], op=ALU.mult)
+            m_a = small.tile([P, P], F32, name="m_a", tag="m_a")
+            nc.gpsimd.tensor_tensor(out=m_a[:], in0=sm[("mean", ct)][:], in1=a_t[:], op=ALU.mult)
+            b_t = small.tile([P, P], F32, name="b_t", tag="b_t", bufs=3)
+            nc.gpsimd.tensor_tensor(out=b_t[:], in0=gb_sb[1][:, ct, :], in1=m_a[:], op=ALU.subtract)
+            sm[("a", ct)] = a_t
+            sm[("b", ct)] = b_t
+
+        def scale_y(e):
+            ct = e // NG
+            wt = work.tile([P, 4, P], F32, name="wt", tag="w")
+            nc.vector.tensor_tensor(
+                out=wt[:],
+                in0=y_t[e][:].rearrange("p (h b) -> p h b", h=4),
+                in1=sm[("a", ct)][:].unsqueeze(1).to_broadcast([P, 4, P]),
+                op=ALU.mult,
+            )
+            w_t[e] = wt
+
+        def finish(e):
+            ct, g = e // NG, e % NG
+            o_ps = ps.tile([P, 4, P], F32, name="o_ps", tag="o", bufs=2)
+            for j in range(4):
+                nc.tensor.matmul(
+                    out=o_ps[:, j, :], lhsT=sm[("b", ct)][:], rhs=ident_f[:], is_transpose=True,
+                    start=True, stop=False,
+                )
+                nc.tensor.matmul(
+                    out=o_ps[:, j, :], lhsT=w_t[e][:, j, :], rhs=ident_f[:], is_transpose=True,
+                    start=False, stop=True,
+                )
+            ot = work.tile([P, 4, P], F32, name="ot", tag="ot", bufs=4)
+            nc.scalar.copy(out=ot[:], in_=o_ps[:])
+            nc.sync.dma_start(out=outv[:, g * 4 : (g + 1) * 4, ct * P : (ct + 1) * P], in_=ot[:])
+
+        def style_turn():
+            dlT_ps = ps.tile([P, 4, P], BF16, name="dlT_ps", tag="f")
+            for kc in range(4):
+                nc.tensor.transpose(dlT_ps[:, kc, :], dl_sb[:, kc * P : (kc + 1) * P], ident_b[:])
+            nc.vector.tensor_copy(out=dlT[:], in_=dlT_ps[:])
+
+        def style_mm(half):
+            gb_ps = ps.tile([P, 4, P], F32, name="gb_ps", tag="o", bufs=2)
             for ct in range(NCT):
                 nt = half * 4 + ct
                 for kc in range(4):
@@ -146,122 +286,60 @@ def tile_styleganlayerepilogue_kernel(
                         start=(kc == 0),
                         stop=(kc == 3),
                     )
+            sm[("gb", half)] = gb_ps
+
+        def style_out(half):
             for ct in range(NCT):
                 col = g1b[:, ct : ct + 1] if half == 0 else cols[:, 12 + ct : 13 + ct]
                 nc.scalar.activation(
-                    out=gb_sb[half][:, ct, :], in_=gb_ps[:, ct, :], func=ACT.Identity, bias=col, scale=1.0
+                    out=gb_sb[half][:, ct, :], in_=sm[("gb", half)][:, ct, :], func=ACT.Identity,
+                    bias=col, scale=1.0,
                 )
 
-        outv = out.rearrange("b h w c -> b (h w) c")
-        y_sb = {}
-        scale_t = {}
-        shift_t = {}
-
-        def phase1(ct):
-            sums = ps.tile([P, 2, P], F32, name="sums", tag="s")
-            sq = []
-            for g in range(NG):
-                acc = ps.tile([P, 512], F32, name="acc", tag="p")
-                nc.tensor.matmul_mx(
-                    out=acc[:],
-                    lhsT=w_codes[:, ct * P : (ct + 1) * P].bitcast(FP8X4),
-                    lhsT_scale=w_scales[:, ct * P : (ct + 1) * P],
-                    rhs=x_codes[g][:].bitcast(FP8X4),
-                    rhs_scale=x_scales[g][:],
-                    start=True,
-                    stop=True,
-                )
-                z = work.tile([P, 512], F32, name="z", tag="z")
-                nc.vector.tensor_tensor(
-                    out=z[:], in0=acc[:], in1=t_add[ct][:, g * 512 : (g + 1) * 512], op=ALU.add
-                )
-                yt = keep.tile([P, 512], F32, name="y%d_%d" % (ct, g))
-                nc.vector.scalar_tensor_tensor(
-                    out=yt[:], in0=z[:], scalar=SLOPE, in1=z[:], op0=ALU.mult, op1=ALU.max
-                )
-                y_sb[(ct, g)] = yt
-                qt = work.tile([P, 512], F32, name="qt", tag="q", bufs=8)
-                nc.scalar.activation(out=qt[:], in_=yt[:], func=ACT.Square)
-                sq.append(qt)
-                for j in range(4):
-                    hw = g * 4 + j
-                    nc.tensor.matmul(
-                        out=sums[:, 0, :],
-                        lhsT=yt[:, j * P : (j + 1) * P],
-                        rhs=ident_f[:],
-                        is_transpose=True,
-                        start=(hw == 0),
-                        stop=(hw == HW - 1),
-                    )
-            for g in range(NG):
-                for j in range(4):
-                    hw = g * 4 + j
-                    nc.tensor.matmul(
-                        out=sums[:, 1, :],
-                        lhsT=sq[g][:, j * P : (j + 1) * P],
-                        rhs=ident_f[:],
-                        is_transpose=True,
-                        start=(hw == 0),
-                        stop=(hw == HW - 1),
-                    )
-            sc = small.tile([P, 2, P], F32, name="sc", tag="sc")
-            nc.scalar.activation(out=sc[:], in_=sums[:], func=ACT.Copy, scale=1.0 / HW)
-            st = ps.tile([P, 2, P], F32, name="st", tag="f")
-            nc.tensor.transpose(st[:, 0, :], sc[:, 0, :], ident_f[:])
-            nc.tensor.transpose(st[:, 1, :], sc[:, 1, :], ident_f[:])
-            msq = small.tile([P, P], F32, name="msq", tag="msq")
-            nc.scalar.activation(out=msq[:], in_=st[:, 0, :], func=ACT.Square)
-            var = small.tile([P, P], F32, name="var", tag="var")
-            nc.vector.tensor_tensor(out=var[:], in0=st[:, 1, :], in1=msq[:], op=ALU.subtract)
-            var2 = small.tile([P, P], F32, name="var2", tag="var2")
-            nc.vector.tensor_scalar(
-                out=var2[:], in0=var[:], scalar1=0.0, scalar2=EPS, op0=ALU.max, op1=ALU.add
-            )
-            sd = small.tile([P, P], F32, name="sd", tag="sd")
-            nc.scalar.sqrt(out=sd[:], in_=var2[:])
-            rstd = small.tile([P, P], F32, name="rstd", tag="rstd")
-            nc.vector.reciprocal(out=rstd[:], in_=sd[:])
-            a_t = small.tile([P, P], F32, name="a_t", tag="a_t")
-            nc.vector.tensor_tensor(out=a_t[:], in0=rstd[:], in1=gb_sb[0][:, ct, :], op=ALU.mult)
-            m_a = small.tile([P, P], F32, name="m_a", tag="m_a")
-            nc.vector.tensor_tensor(out=m_a[:], in0=st[:, 0, :], in1=a_t[:], op=ALU.mult)
-            b_t = small.tile([P, P], F32, name="b_t", tag="b_t")
-            nc.vector.tensor_tensor(out=b_t[:], in0=gb_sb[1][:, ct, :], in1=m_a[:], op=ALU.subtract)
-            scale_t[ct] = a_t
-            shift_t[ct] = b_t
-
-        def phase2(ct):
-            a_t = scale_t[ct]
-            b_t = shift_t[ct]
-            for g in range(NG):
-                wt = work.tile([P, 4, P], F32, name="wt", tag="w")
-                nc.vector.tensor_tensor(
-                    out=wt[:],
-                    in0=y_sb[(ct, g)][:].rearrange("p (h b) -> p h b", h=4),
-                    in1=a_t[:].unsqueeze(1).to_broadcast([P, 4, P]),
-                    op=ALU.mult,
-                )
-                o_ps = ps.tile([P, 4, P], F32, name="o_ps", tag="o")
-                for j in range(4):
-                    nc.tensor.matmul(
-                        out=o_ps[:, j, :], lhsT=b_t[:], rhs=ident_f[:], is_transpose=True,
-                        start=True, stop=False,
-                    )
-                    nc.tensor.matmul(
-                        out=o_ps[:, j, :], lhsT=wt[:, j, :], rhs=ident_f[:], is_transpose=True,
-                        start=False, stop=True,
-                    )
-                ot = work.tile([P, 4, P], F32, name="ot", tag="ot", bufs=4)
-                nc.scalar.copy(out=ot[:], in_=o_ps[:])
-                nc.sync.dma_start(
-                    out=outv[:, g * 4 : (g + 1) * 4, ct * P : (ct + 1) * P], in_=ot[:]
-                )
-
-        phase1(0)
-        phase1(1)
-        phase2(0)
-        phase1(2)
-        phase2(1)
-        phase1(3)
-        phase2(2)
-        phase2(3)
+        x_turn(0)
+        x_quant(0)
+        mx(0)
+        for i in range(NSTEP + LAG + 2):
+            rel = [(ct, i - (NG * ct + NG - 1)) for ct in range(NCT)]
+            if i + 1 < NG:
+                x_turn(i + 1)
+            if i == 6:
+                style_out(1)
+            for ct, r in rel:
+                if r == 2:
+                    stats_a(ct)
+                if r == 3:
+                    stats_c(ct)
+            if i < NSTEP:
+                zy(i)
+            if i + 1 < NG:
+                x_quant(i + 1)
+            if 1 <= i <= NSTEP:
+                sums(i - 1)
+            for ct, r in rel:
+                if r == 1:
+                    stats_scale(ct)
+            if i + 1 < NG:
+                mx(i + 1)
+            if i >= 2 and i % 2 == 0 and i + 3 < NSTEP:
+                mx(i + 2, 1 + EXTRA_MX)
+                mx(i + 3)
+            if i < NSTEP:
+                square(i)
+            for ct, r in rel:
+                if r == 2:
+                    stats_b(ct)
+            if 0 <= i - LAG < NSTEP:
+                scale_y(i - LAG)
+            if 0 <= i - LAG - 1 < NSTEP:
+                finish(i - LAG - 1)
+            for ct, r in rel:
+                if r == 1:
+                    stats_turn(ct)
+            if i == 3:
+                style_turn()
+            if i == 4:
+                style_mm(0)
+            if i == 5:
+                style_out(0)
+                style_mm(1)

@@ -21,7 +21,7 @@ NSTEP = NG * NCT
 EPS = 1e-8
 SLOPE = 0.2
 LAG = 8
-EXTRA_MX = 0
+EXTRA_MX = 1
 
 
 def tile_styleganlayerepilogue_kernel(
@@ -321,9 +321,8 @@ def tile_styleganlayerepilogue_kernel(
                     stats_scale(ct)
             if i + 1 < NG:
                 mx(i + 1)
-            if i >= 2 and i % 2 == 0 and i + 3 < NSTEP:
+            if i >= 2 and i + 2 < NSTEP:
                 mx(i + 2, 1 + EXTRA_MX)
-                mx(i + 3)
             if i < NSTEP:
                 square(i)
             for ct, r in rel:

@@ -9,6 +9,7 @@ F32 = mybir.dt.float32
 BF16 = mybir.dt.bfloat16
 U32 = mybir.dt.uint32
 U8 = mybir.dt.uint8
+I32 = mybir.dt.int32
 FP8X4 = mybir.dt.float8_e4m3fn_x4
 ALU = mybir.AluOpType
 ACT = mybir.ActivationFunctionType
@@ -21,7 +22,7 @@ NSTEP = NG * NCT
 EPS = 1e-8
 SLOPE = 0.2
 LAG = 8
-EXTRA_MX = 1
+EXTRA_MX = 0
 
 
 def tile_styleganlayerepilogue_kernel(
@@ -36,13 +37,13 @@ def tile_styleganlayerepilogue_kernel(
         ctx.enter_context(tc.manual_schedule())
 
         rows = keep.tile([P, P], BF16, name="rows")
-        nc.gpsimd.memset(rows[:], 0.0)
+        nc.vector.memset(rows[:].bitcast(I32), 0)
+        warm = keep.tile([P, 1], F32, name="warm")
+        nc.vector.memset(warm[:], 1.0)
         ident_b = keep.tile([P, P], BF16, name="ident_b")
         make_identity(nc, ident_b[:])
         ident_f = keep.tile([P, P], F32, name="ident_f")
         make_identity(nc, ident_f[:])
-        warm = keep.tile([P, 1], F32, name="warm")
-        nc.vector.memset(warm[:], 1.0)
         warm2 = keep.tile([P, 1], F32, name="warm2")
 
         xv = x.rearrange("b h w c -> b (h w c)")
@@ -52,31 +53,34 @@ def tile_styleganlayerepilogue_kernel(
         dl_sb = keep.tile([P, 512], BF16, name="dl_sb")
         dw_sb = keep.tile([P, 4, 1024], BF16, name="dw_sb")
 
-        nc.scalar.dma_start(out=nm_sb[:], in_=noise_map.rearrange("b h w o -> b (h w o)"))
-        nc.scalar.dma_start(
+        nc.sync.dma_start(out=nm_sb[:], in_=noise_map.rearrange("b h w o -> b (h w o)"))
+        nc.sync.dma_start(
             out=rows[0:4, :], in_=noise_weight.rearrange("a b c (r n) -> (a b c r) n", r=4)
         )
-        nc.scalar.dma_start(out=rows[4:8, :], in_=bias.rearrange("a b c (r n) -> (a b c r) n", r=4))
-        nc.scalar.dma_start(out=rows[8:16, :], in_=dense_b.rearrange("(r n) -> r n", r=8))
+        nc.sync.dma_start(out=rows[4:8, :], in_=bias.rearrange("a b c (r n) -> (a b c r) n", r=4))
         nc.scalar.sqrt(out=warm2[:], in_=warm[:])
+        nc.sync.dma_start(out=x_sb[0][:], in_=xv[:, 0:2048])
         nc.sync.dma_start(
             out=w_raw[:].rearrange("p (u e) c -> p u (e c)", u=2),
             in_=conv_w.rearrange("(u q e) c -> q u (e c)", u=2, e=2),
         )
-        for g in range(NG):
+        for g in range(1, NG):
             nc.sync.dma_start(out=x_sb[g][:], in_=xv[:, g * 2048 : (g + 1) * 2048])
         nc.sync.dma_start(out=dl_sb[:], in_=dlatents)
         nc.sync.dma_start(out=dw_sb[:], in_=dense_w.rearrange("(k p) n -> p k n", p=P))
+        db_bc = keep.tile([P, 1024], BF16, name="db_bc")
+        nc.sync.dma_start(out=db_bc[:], in_=dense_b.partition_broadcast(P))
 
-        cols_ps = ps.tile([P, P], BF16, name="cols_ps", tag="f")
+        cols_ps = ps.tile([P, P], BF16, name="cols_ps", tag="a", bufs=2)
         nc.tensor.transpose(cols_ps[:], rows[:], ident_b[:])
-        cols = keep.tile([P, 16], F32, name="cols")
-        nc.vector.tensor_copy(out=cols[:], in_=cols_ps[:, 0:16])
-        g1b = keep.tile([P, 4], F32, name="g1b")
-        nc.vector.tensor_scalar_add(out=g1b[:], in0=cols[:, 8:12], scalar1=1.0)
+        cols = keep.tile([P, 8], F32, name="cols")
+        nc.vector.tensor_copy(out=cols[:], in_=cols_ps[:, 0:8])
+
 
         nm_bc = [keep.tile([P, 1024], BF16, name="nm_bc%d" % h) for h in range(2)]
-        for half in range(2):
+        t_add = {}
+
+        def noise_half(half):
             nm_ps = ps.tile([P, 1024], BF16, name="nm_ps%d" % half, tag=("sy" if half == 0 else "sq"))
             for j in range(8):
                 hw = half * 8 + j
@@ -89,8 +93,7 @@ def tile_styleganlayerepilogue_kernel(
                 )
             nc.scalar.copy(out=nm_bc[half][:], in_=nm_ps[:])
 
-        t_add = {}
-        for s in range(NSTEP):
+        def noise_term(s):
             ct, g = s // NG, s % NG
             t_add[s] = keep.tile([P, 512], F32, name="t_add%d" % s)
             nc.gpsimd.tensor_scalar(
@@ -102,35 +105,49 @@ def tile_styleganlayerepilogue_kernel(
                 op1=ALU.add,
             )
 
+        def noise_term_s(s):
+            ct, g = s // NG, s % NG
+            t_add[s] = keep.tile([P, 512], F32, name="t_add%d" % s)
+            nc.scalar.activation(
+                out=t_add[s][:],
+                in_=nm_bc[g // 2][:, (g % 2) * 512 : (g % 2 + 1) * 512],
+                func=ACT.Identity,
+                bias=cols[:, 4 + ct : 5 + ct],
+                scale=cols[:, ct : ct + 1],
+            )
+
         w_grp = keep.tile([P, 512, 4], BF16, name="w_grp", align_bytes=64)
         w_codes = keep.tile([P, 512], U32, name="w_codes", align_bytes=64)
         w_scales = keep.tile([P, 512], U8, name="w_scales", align_bytes=64)
-        nc.vector.tensor_copy(out=w_grp[:], in_=w_raw[:].rearrange("p t c -> p c t"))
-        nc.vector.quantize_mx(
-            out=w_codes[:].bitcast(FP8X4),
-            scales=w_scales[:],
-            in_=w_grp[:].rearrange("p c t -> p (c t)"),
-        )
+
+        def w_quant():
+            nc.vector.tensor_copy(out=w_grp[:], in_=w_raw[:].rearrange("p t c -> p c t"))
+            nc.vector.quantize_mx(
+                out=w_codes[:].bitcast(FP8X4),
+                scales=w_scales[:],
+                in_=w_grp[:].rearrange("p c t -> p (c t)"),
+            )
 
         x_grp = [keep.tile([P, 2048], BF16, name="x_grp%d" % g, align_bytes=64) for g in range(NG)]
         x_codes = [keep.tile([P, 512], U32, name="x_codes%d" % g, align_bytes=64) for g in range(NG)]
         x_scales = [keep.tile([P, 512], U8, name="x_scales%d" % g, align_bytes=64) for g in range(NG)]
         outv = out.rearrange("b h w c -> b (h w) c")
         acc_t = {}
+        z_t = {}
         y_t = {}
         q_t = {}
         w_t = {}
         sum_t = {}
         st_t = {}
         sm = {}
-        gb_sb = [keep.tile([P, 4, P], F32, name="gb_sb%d" % h) for h in range(2)]
+        gb_sb = [keep.tile([P, 512], F32, name="gb_sb%d" % h) for h in range(2)]
         dlT = keep.tile([P, 4, P], BF16, name="dlT")
 
-        def x_turn(g):
+        def x_turn(g, tag):
             xw = x_sb[g][:].bitcast(F32)
             xgw = x_grp[g][:].bitcast(F32)
             for hh in range(2):
-                xt = ps.tile([P, 4, P], F32, name="xt", tag="o", bufs=2)
+                xt = ps.tile([P, 4, P], F32, name="xt", tag=tag, bufs=2)
                 for j in range(4):
                     col = (hh * 2 + j // 2) * 256 + (j % 2) * P
                     nc.tensor.transpose(xt[:, j, :], xw[:, col : col + P], ident_f[:])
@@ -148,7 +165,7 @@ def tile_styleganlayerepilogue_kernel(
 
         def mx(s, times=1):
             ct, g = s // NG, s % NG
-            acc = ps.tile([P, 512], F32, name="acc", tag="p", bufs=3)
+            acc = ps.tile([P, 512], F32, name="acc", tag="p", bufs=2)
             for rep in range(times):
                 nc.tensor.matmul_mx(
                     out=acc[:],
@@ -161,9 +178,13 @@ def tile_styleganlayerepilogue_kernel(
                 )
             acc_t[s] = acc
 
-        def zy(s):
+        def z_only(s):
             z = work.tile([P, 512], F32, name="z", tag="z")
             nc.vector.tensor_tensor(out=z[:], in0=acc_t[s][:], in1=t_add[s][:], op=ALU.add)
+            z_t[s] = z
+
+        def y_only(s):
+            z = z_t[s]
             yt = keep.tile([P, 512], F32, name="y%d" % s)
             nc.vector.scalar_tensor_tensor(
                 out=yt[:], in0=z[:], scalar=SLOPE, in1=z[:], op0=ALU.mult, op1=ALU.max
@@ -175,18 +196,17 @@ def tile_styleganlayerepilogue_kernel(
             nc.scalar.activation(out=qt[:], in_=y_t[s][:], func=ACT.Square)
             q_t[s] = qt
 
-        def sums(s):
+        def sums(s, k):
             ct, g = s // NG, s % NG
             if g == 0:
-                sum_y = ps.tile([P, P], F32, name="sum_y", tag="sy")
-                sum_q = ps.tile([P, P], F32, name="sum_q", tag="sq")
-                sum_t[ct] = (sum_y, sum_q)
-            for k in range(2):
+                acc_sum = ps.tile([P, P], F32, name="acc_sum", tag=("sy" if k == 0 else "sq"))
+                sum_t[(ct, k)] = acc_sum
+            if True:
                 src = y_t[s] if k == 0 else q_t[s]
                 for j in range(4):
                     hw = g * 4 + j
                     nc.tensor.matmul(
-                        out=sum_t[ct][k][:],
+                        out=sum_t[(ct, k)][:],
                         lhsT=src[:, j * P : (j + 1) * P],
                         rhs=ident_f[:],
                         is_transpose=True,
@@ -194,32 +214,19 @@ def tile_styleganlayerepilogue_kernel(
                         stop=(hw == HW - 1),
                     )
 
-        def stats_scale(ct):
-            sc = small.tile([P, 2, P], F32, name="sc", tag="sc")
-            for k in range(2):
-                nc.scalar.activation(
-                    out=sc[:, k, :], in_=sum_t[ct][k][:], func=ACT.Copy, scale=1.0 / HW
-                )
-            sm[("sc", ct)] = sc
-
-        def stats_turn(ct):
-            st = ps.tile([P, 2, P], F32, name="st", tag="f")
-            for k in range(2):
-                nc.tensor.transpose(st[:, k, :], sm[("sc", ct)][:, k, :], ident_f[:])
-            st_t[ct] = st
-
         def stats_a(ct):
-            msq = small.tile([P, P], F32, name="msq", tag="msq")
-            nc.scalar.activation(out=msq[:], in_=st_t[ct][:, 0, :], func=ACT.Square)
             mean = small.tile([P, P], F32, name="mean", tag="mean")
-            nc.scalar.copy(out=mean[:], in_=st_t[ct][:, 0, :])
+            nc.scalar.activation(out=mean[:], in_=sum_t[(ct, 0)][:], func=ACT.Copy, scale=1.0 / HW)
+            msq = small.tile([P, P], F32, name="msq", tag="msq")
+            nc.scalar.activation(out=msq[:], in_=sum_t[(ct, 0)][:], func=ACT.Square, scale=1.0 / HW)
             sm[("msq", ct)] = msq
             sm[("mean", ct)] = mean
 
         def stats_b(ct):
             var = small.tile([P, P], F32, name="var", tag="var")
-            nc.vector.tensor_tensor(
-                out=var[:], in0=st_t[ct][:, 1, :], in1=sm[("msq", ct)][:], op=ALU.subtract
+            nc.vector.scalar_tensor_tensor(
+                out=var[:], in0=sum_t[(ct, 1)][:], scalar=1.0 / HW, in1=sm[("msq", ct)][:],
+                op0=ALU.mult, op1=ALU.subtract,
             )
             var2 = small.tile([P, P], F32, name="var2", tag="var2")
             nc.vector.tensor_scalar(
@@ -230,20 +237,26 @@ def tile_styleganlayerepilogue_kernel(
             sm[("sd", ct)] = sd
 
         def stats_c(ct):
+            cs = slice(ct * P, (ct + 1) * P)
             rstd = small.tile([P, P], F32, name="rstd", tag="rstd")
             nc.vector.reciprocal(out=rstd[:], in_=sm[("sd", ct)][:])
-            a_t = small.tile([P, P], F32, name="a_t", tag="a_t", bufs=3)
-            nc.vector.tensor_tensor(out=a_t[:], in0=rstd[:], in1=gb_sb[0][:, ct, :], op=ALU.mult)
+            a_c = small.tile([P, P], F32, name="a_c", tag="a_c")
+            nc.vector.tensor_tensor(out=a_c[:], in0=rstd[:], in1=gb_sb[0][:, cs], op=ALU.mult)
+            sm[("ac", ct)] = a_c
             m_a = small.tile([P, P], F32, name="m_a", tag="m_a")
-            nc.gpsimd.tensor_tensor(out=m_a[:], in0=sm[("mean", ct)][:], in1=a_t[:], op=ALU.mult)
-            b_t = small.tile([P, P], F32, name="b_t", tag="b_t", bufs=3)
-            nc.gpsimd.tensor_tensor(out=b_t[:], in0=gb_sb[1][:, ct, :], in1=m_a[:], op=ALU.subtract)
-            sm[("a", ct)] = a_t
-            sm[("b", ct)] = b_t
+            nc.gpsimd.tensor_tensor(out=m_a[:], in0=sm[("mean", ct)][:], in1=a_c[:], op=ALU.mult)
+            b_c = small.tile([P, P], F32, name="b_c", tag="b_c", bufs=3)
+            nc.gpsimd.tensor_tensor(out=b_c[:], in0=gb_sb[1][:, cs], in1=m_a[:], op=ALU.subtract)
+            sm[("b", ct)] = b_c
+
+        def stats_d(ct):
+            a_ps = ps.tile([P, P], F32, name="a_ps", tag="a", bufs=2)
+            nc.tensor.transpose(a_ps[:], sm[("ac", ct)][:], ident_f[:])
+            sm[("a", ct)] = a_ps
 
         def scale_y(e):
             ct = e // NG
-            wt = work.tile([P, 4, P], F32, name="wt", tag="w")
+            wt = work.tile([P, 4, P], F32, name="wt", tag="w", bufs=4)
             nc.vector.tensor_tensor(
                 out=wt[:],
                 in0=y_t[e][:].rearrange("p (h b) -> p h b", h=4),
@@ -252,93 +265,127 @@ def tile_styleganlayerepilogue_kernel(
             )
             w_t[e] = wt
 
-        def finish(e):
-            ct, g = e // NG, e % NG
-            o_ps = ps.tile([P, 4, P], F32, name="o_ps", tag="o", bufs=2)
+        def turn_out(e, tag="o"):
+            o_ps = ps.tile([P, 4, P], F32, name="o_ps", tag=tag, bufs=2)
             for j in range(4):
-                nc.tensor.matmul(
-                    out=o_ps[:, j, :], lhsT=sm[("b", ct)][:], rhs=ident_f[:], is_transpose=True,
-                    start=True, stop=False,
-                )
-                nc.tensor.matmul(
-                    out=o_ps[:, j, :], lhsT=w_t[e][:, j, :], rhs=ident_f[:], is_transpose=True,
-                    start=False, stop=True,
-                )
-            ot = work.tile([P, 4, P], F32, name="ot", tag="ot", bufs=4)
-            nc.scalar.copy(out=ot[:], in_=o_ps[:])
+                nc.tensor.transpose(o_ps[:, j, :], w_t[e][:, j, :], ident_f[:])
+            sm[("o", e)] = o_ps
+
+        def shift_store(e):
+            ct, g = e // NG, e % NG
+            ot = work.tile([P, 4, P], F32, name="ot", tag="ot", bufs=8)
+            nc.vector.tensor_tensor(
+                out=ot[:],
+                in0=sm[("o", e)][:],
+                in1=sm[("b", ct)][:].unsqueeze(1).to_broadcast([P, 4, P]),
+                op=ALU.add,
+            )
             nc.sync.dma_start(out=outv[:, g * 4 : (g + 1) * 4, ct * P : (ct + 1) * P], in_=ot[:])
 
         def style_turn():
-            dlT_ps = ps.tile([P, 4, P], BF16, name="dlT_ps", tag="f")
+            dlT_ps = ps.tile([P, 4, P], BF16, name="dlT_ps", tag="a", bufs=2)
             for kc in range(4):
                 nc.tensor.transpose(dlT_ps[:, kc, :], dl_sb[:, kc * P : (kc + 1) * P], ident_b[:])
             nc.vector.tensor_copy(out=dlT[:], in_=dlT_ps[:])
 
         def style_mm(half):
-            gb_ps = ps.tile([P, 4, P], F32, name="gb_ps", tag="o", bufs=2)
-            for ct in range(NCT):
-                nt = half * 4 + ct
-                for kc in range(4):
-                    nc.tensor.matmul(
-                        out=gb_ps[:, ct, :],
-                        lhsT=dw_sb[:, kc, nt * P : (nt + 1) * P],
-                        rhs=dlT[:, kc, :],
-                        start=(kc == 0),
-                        stop=(kc == 3),
-                    )
+            gb_ps = ps.tile([P, 512], F32, name="gb_ps", tag="o", bufs=2)
+            for kc in range(4):
+                nc.tensor.matmul(
+                    out=gb_ps[:],
+                    lhsT=dlT[:, kc, :],
+                    rhs=dw_sb[:, kc, half * 512 : (half + 1) * 512],
+                    start=(kc == 0),
+                    stop=(kc == 3),
+                )
             sm[("gb", half)] = gb_ps
 
         def style_out(half):
-            for ct in range(NCT):
-                col = g1b[:, ct : ct + 1] if half == 0 else cols[:, 12 + ct : 13 + ct]
-                nc.scalar.activation(
-                    out=gb_sb[half][:, ct, :], in_=sm[("gb", half)][:, ct, :], func=ACT.Identity,
-                    bias=col, scale=1.0,
-                )
+            nc.vector.scalar_tensor_tensor(
+                out=gb_sb[half][:], in0=sm[("gb", half)][:], scalar=(1.0 if half == 0 else 0.0),
+                in1=db_bc[:, half * 512 : (half + 1) * 512], op0=ALU.add, op1=ALU.add,
+            )
 
-        x_turn(0)
+        noise_half(0)
+        x_turn(0, "o")
+        noise_half(1)
+        for s in range(NG):
+            noise_term(s)
+        w_quant()
+        x_turn(1, "p")
         x_quant(0)
+        x_turn(2, "o")
         mx(0)
-        for i in range(NSTEP + LAG + 2):
+        x_quant(1)
+        x_turn(3, "o")
+        mx(1)
+        for i in range(NSTEP):
             rel = [(ct, i - (NG * ct + NG - 1)) for ct in range(NCT)]
-            if i + 1 < NG:
-                x_turn(i + 1)
-            if i == 6:
-                style_out(1)
             for ct, r in rel:
                 if r == 2:
                     stats_a(ct)
+            if i - LAG - 2 >= 0:
+                shift_store(i - LAG - 2)
+            if i == 6:
+                style_out(0)
+                style_out(1)
+            for ct, r in rel:
                 if r == 3:
-                    stats_c(ct)
-            if i < NSTEP:
-                zy(i)
-            if i + 1 < NG:
-                x_quant(i + 1)
-            if 1 <= i <= NSTEP:
-                sums(i - 1)
-            for ct, r in rel:
-                if r == 1:
-                    stats_scale(ct)
-            if i + 1 < NG:
-                mx(i + 1)
-            if i >= 2 and i + 2 < NSTEP:
-                mx(i + 2, 1 + EXTRA_MX)
-            if i < NSTEP:
-                square(i)
-            for ct, r in rel:
-                if r == 2:
                     stats_b(ct)
-            if 0 <= i - LAG < NSTEP:
-                scale_y(i - LAG)
-            if 0 <= i - LAG - 1 < NSTEP:
-                finish(i - LAG - 1)
             for ct, r in rel:
-                if r == 1:
-                    stats_turn(ct)
+                if r == 4:
+                    stats_c(ct)
+            if i - LAG - 1 >= 0:
+                turn_out(i - LAG - 1)
+            if i >= 2:
+                sums(i - 2, 1)
+            z_only(i)
+            if i + 2 < NG:
+                x_quant(i + 2)
+            if i - LAG >= 0:
+                scale_y(i - LAG)
+            y_only(i)
+            if i >= 1:
+                sums(i - 1, 0)
+            for ct, r in rel:
+                if r == 4:
+                    stats_d(ct)
+            if i + 2 < NSTEP:
+                mx(i + 2)
+            if i + NG < NSTEP:
+                noise_term_s(i + NG)
+            square(i)
             if i == 3:
                 style_turn()
             if i == 4:
                 style_mm(0)
-            if i == 5:
-                style_out(0)
                 style_mm(1)
+        last = NCT - 1
+        a0 = NSTEP - LAG
+        sums(NSTEP - 1, 0)
+        sums(NSTEP - 2, 1)
+        stats_a(last)
+        shift_store(a0 - 2)
+        turn_out(a0 - 1)
+        scale_y(a0)
+        sums(NSTEP - 1, 1)
+        scale_y(a0 + 1)
+        shift_store(a0 - 1)
+        turn_out(a0, "p")
+        stats_b(last)
+        scale_y(a0 + 2)
+        turn_out(a0 + 1, "p")
+        scale_y(a0 + 3)
+        shift_store(a0)
+        turn_out(a0 + 2)
+        stats_c(last)
+        stats_d(last)
+        shift_store(a0 + 1)
+        turn_out(a0 + 3)
+        shift_store(a0 + 2)
+        shift_store(a0 + 3)
+        for k in range(NG):
+            scale_y(a0 + 4 + k)
+            turn_out(a0 + 4 + k, "p" if k < 2 else "o")
+        for k in range(NG):
+            shift_store(a0 + 4 + k)

@@ -22,7 +22,7 @@ NSTEP = NG * NCT
 EPS = 1e-8
 SLOPE = 0.2
 LAG = 8
-EXTRA_MX = 0
+USE_SG = True
 
 
 def tile_styleganlayerepilogue_kernel(
@@ -45,6 +45,8 @@ def tile_styleganlayerepilogue_kernel(
         ident_f = keep.tile([P, P], F32, name="ident_f")
         make_identity(nc, ident_f[:])
         warm2 = keep.tile([P, 1], F32, name="warm2")
+        eps_t = keep.tile([P, 1], F32, name="eps_t")
+        nc.vector.memset(eps_t[:], EPS)
 
         xv = x.rearrange("b h w c -> b (h w c)")
         x_sb = [keep.tile([P, 2048], BF16, name="x_sb%d" % g) for g in range(NG)]
@@ -58,7 +60,7 @@ def tile_styleganlayerepilogue_kernel(
             out=rows[0:4, :], in_=noise_weight.rearrange("a b c (r n) -> (a b c r) n", r=4)
         )
         nc.sync.dma_start(out=rows[4:8, :], in_=bias.rearrange("a b c (r n) -> (a b c r) n", r=4))
-        nc.scalar.sqrt(out=warm2[:], in_=warm[:])
+        nc.scalar.activation(out=warm2[:], in_=warm[:], func=ACT.Abs_reciprocal_sqrt)
         nc.sync.dma_start(out=x_sb[0][:], in_=xv[:, 0:2048])
         nc.sync.dma_start(
             out=w_raw[:].rearrange("p (u e) c -> p u (e c)", u=2),
@@ -228,18 +230,15 @@ def tile_styleganlayerepilogue_kernel(
                 out=var[:], in0=sum_t[(ct, 1)][:], scalar=1.0 / HW, in1=sm[("msq", ct)][:],
                 op0=ALU.mult, op1=ALU.subtract,
             )
-            var2 = small.tile([P, P], F32, name="var2", tag="var2")
-            nc.vector.tensor_scalar(
-                out=var2[:], in0=var[:], scalar1=0.0, scalar2=EPS, op0=ALU.max, op1=ALU.add
+            rstd = small.tile([P, P], F32, name="rstd", tag="rstd")
+            nc.scalar.activation(
+                out=rstd[:], in_=var[:], func=ACT.Abs_reciprocal_sqrt, bias=eps_t[:], scale=1.0
             )
-            sd = small.tile([P, P], F32, name="sd", tag="sd")
-            nc.scalar.sqrt(out=sd[:], in_=var2[:])
-            sm[("sd", ct)] = sd
+            sm[("rstd", ct)] = rstd
 
         def stats_c(ct):
             cs = slice(ct * P, (ct + 1) * P)
-            rstd = small.tile([P, P], F32, name="rstd", tag="rstd")
-            nc.vector.reciprocal(out=rstd[:], in_=sm[("sd", ct)][:])
+            rstd = sm[("rstd", ct)]
             a_c = small.tile([P, P], F32, name="a_c", tag="a_c")
             nc.vector.tensor_tensor(out=a_c[:], in0=rstd[:], in1=gb_sb[0][:, cs], op=ALU.mult)
             sm[("ac", ct)] = a_c
@@ -281,6 +280,25 @@ def tile_styleganlayerepilogue_kernel(
                 op=ALU.add,
             )
             nc.sync.dma_start(out=outv[:, g * 4 : (g + 1) * 4, ct * P : (ct + 1) * P], in_=ot[:])
+
+        def shift_store_sg(e):
+            ct, g = e // NG, e % NG
+            ev = work.tile([P, 4, P], F32, name="ev", tag="ev")
+            nc.scalar.copy(out=ev[:], in_=sm[("o", e)][:])
+            ot = work.tile([P, 4, P], F32, name="ot", tag="ot", bufs=8)
+            nc.gpsimd.tensor_tensor(
+                out=ot[:],
+                in0=ev[:],
+                in1=sm[("b", ct)][:].unsqueeze(1).to_broadcast([P, 4, P]),
+                op=ALU.add,
+            )
+            nc.sync.dma_start(out=outv[:, g * 4 : (g + 1) * 4, ct * P : (ct + 1) * P], in_=ot[:])
+
+        def shift(e):
+            if e < 12 and e % 2 == 1 and USE_SG:
+                shift_store_sg(e)
+            else:
+                shift_store(e)
 
         def style_turn():
             dlT_ps = ps.tile([P, 4, P], BF16, name="dlT_ps", tag="a", bufs=2)
@@ -325,7 +343,7 @@ def tile_styleganlayerepilogue_kernel(
                 if r == 2:
                     stats_a(ct)
             if i - LAG - 2 >= 0:
-                shift_store(i - LAG - 2)
+                shift(i - LAG - 2)
             if i == 6:
                 style_out(0)
                 style_out(1)
@@ -361,31 +379,30 @@ def tile_styleganlayerepilogue_kernel(
                 style_mm(0)
                 style_mm(1)
         last = NCT - 1
-        a0 = NSTEP - LAG
         sums(NSTEP - 1, 0)
         sums(NSTEP - 2, 1)
         stats_a(last)
-        shift_store(a0 - 2)
-        turn_out(a0 - 1)
-        scale_y(a0)
+        shift(6)
+        scale_y(8)
+        turn_out(7, "o")
         sums(NSTEP - 1, 1)
-        scale_y(a0 + 1)
-        shift_store(a0 - 1)
-        turn_out(a0, "p")
+        shift(7)
+        scale_y(9)
+        turn_out(8, "p")
         stats_b(last)
-        scale_y(a0 + 2)
-        turn_out(a0 + 1, "p")
-        scale_y(a0 + 3)
-        shift_store(a0)
-        turn_out(a0 + 2)
+        shift(8)
+        scale_y(10)
+        turn_out(9, "p")
+        shift(9)
+        scale_y(11)
+        turn_out(10, "o")
         stats_c(last)
         stats_d(last)
-        shift_store(a0 + 1)
-        turn_out(a0 + 3)
-        shift_store(a0 + 2)
-        shift_store(a0 + 3)
+        shift(10)
+        turn_out(11, "o")
+        shift(11)
         for k in range(NG):
-            scale_y(a0 + 4 + k)
-            turn_out(a0 + 4 + k, "p" if k < 2 else "o")
+            scale_y(12 + k)
+            turn_out(12 + k, "p" if k < 2 else "o")
         for k in range(NG):
-            shift_store(a0 + 4 + k)
+            shift(12 + k)

@@ -34,7 +34,6 @@ def tile_styleganlayerepilogue_kernel(
         work = ctx.enter_context(tc.tile_pool(name="work", bufs=3))
         small = ctx.enter_context(tc.tile_pool(name="small", bufs=2))
         ps = ctx.enter_context(tc.psum_pool(name="ps", bufs=1))
-        ctx.enter_context(tc.manual_schedule())
 
         rows = keep.tile([P, P], BF16, name="rows")
         nc.vector.memset(rows[:].bitcast(I32), 0)

from contextlib import ExitStack

import concourse.mybir as mybir
from concourse.masks import make_identity

FLOPS = 2 * 2048 * 512 * 512 + 2 * 128 * 512 * 1024

F32 = mybir.dt.float32
BF16 = mybir.dt.bfloat16
U32 = mybir.dt.uint32
U8 = mybir.dt.uint8
I32 = mybir.dt.int32
FP8X4 = mybir.dt.float8_e4m3fn_x4
ALU = mybir.AluOpType
ACT = mybir.ActivationFunctionType

P = 128
HW = 16
NG = 4
NCT = 4
NSTEP = NG * NCT
EPS = 1e-8
SLOPE = 0.2
LAG = 8
USE_SG = True


def tile_styleganlayerepilogue_kernel(
    tc, x, dlatents, noise_map, conv_w, noise_weight, bias, dense_w, dense_b, out
):
    nc = tc.nc
    with ExitStack() as ctx:
        keep = ctx.enter_context(tc.tile_pool(name="keep", bufs=1))
        work = ctx.enter_context(tc.tile_pool(name="work", bufs=3))
        small = ctx.enter_context(tc.tile_pool(name="small", bufs=2))
        ps = ctx.enter_context(tc.psum_pool(name="ps", bufs=1))

        rows = keep.tile([P, P], BF16, name="rows")
        nc.vector.memset(rows[:].bitcast(I32), 0)
        warm = keep.tile([P, 1], F32, name="warm")
        nc.vector.memset(warm[:], 1.0)
        ident_b = keep.tile([P, P], BF16, name="ident_b")
        make_identity(nc, ident_b[:])
        ident_f = keep.tile([P, P], F32, name="ident_f")
        make_identity(nc, ident_f[:])
        warm2 = keep.tile([P, 1], F32, name="warm2")
        eps_t = keep.tile([P, 1], F32, name="eps_t")
        nc.vector.memset(eps_t[:], EPS)

        xv = x.rearrange("b h w c -> b (h w c)")
        x_sb = [keep.tile([P, 2048], BF16, name="x_sb%d" % g) for g in range(NG)]
        w_raw = keep.tile([P, 4, 512], BF16, name="w_raw")
        nm_sb = keep.tile([P, HW], BF16, name="nm_sb")
        dl_sb = keep.tile([P, 512], BF16, name="dl_sb")
        dw_sb = keep.tile([P, 4, 1024], BF16, name="dw_sb")

        nc.sync.dma_start(out=nm_sb[:], in_=noise_map.rearrange("b h w o -> b (h w o)"))
        nc.sync.dma_start(
            out=rows[0:4, :], in_=noise_weight.rearrange("a b c (r n) -> (a b c r) n", r=4)
        )
        nc.sync.dma_start(out=rows[4:8, :], in_=bias.rearrange("a b c (r n) -> (a b c r) n", r=4))
        nc.scalar.activation(out=warm2[:], in_=warm[:], func=ACT.Abs_reciprocal_sqrt)
        nc.sync.dma_start(out=x_sb[0][:], in_=xv[:, 0:2048])
        nc.sync.dma_start(
            out=w_raw[:].rearrange("p (u e) c -> p u (e c)", u=2),
            in_=conv_w.rearrange("(u q e) c -> q u (e c)", u=2, e=2),
        )
        for g in range(1, NG):
            nc.sync.dma_start(out=x_sb[g][:], in_=xv[:, g * 2048 : (g + 1) * 2048])
        nc.sync.dma_start(out=dl_sb[:], in_=dlatents)
        nc.sync.dma_start(out=dw_sb[:], in_=dense_w.rearrange("(k p) n -> p k n", p=P))
        db_bc = keep.tile([P, 1024], BF16, name="db_bc")
        nc.sync.dma_start(out=db_bc[:], in_=dense_b.partition_broadcast(P))

        cols_ps = ps.tile([P, P], BF16, name="cols_ps", tag="a", bufs=2)
        nc.tensor.transpose(cols_ps[:], rows[:], ident_b[:])
        cols = keep.tile([P, 8], F32, name="cols")
        nc.vector.tensor_copy(out=cols[:], in_=cols_ps[:, 0:8])


        nm_bc = [keep.tile([P, 1024], BF16, name="nm_bc%d" % h) for h in range(2)]
        t_add = {}

        def noise_half(half):
            nm_ps = ps.tile([P, 1024], BF16, name="nm_ps%d" % half, tag=("sy" if half == 0 else "sq"))
            for j in range(8):
                hw = half * 8 + j
                nc.tensor.matmul(
                    out=nm_ps[:, j * P : (j + 1) * P],
                    lhsT=nm_sb[:, hw : hw + 1].to_broadcast([P, P]),
                    rhs=ident_b[:],
                    start=True,
                    stop=True,
                )
            nc.scalar.copy(out=nm_bc[half][:], in_=nm_ps[:])

        def noise_term(s):
            ct, g = s // NG, s % NG
            t_add[s] = keep.tile([P, 512], F32, name="t_add%d" % s)
            nc.gpsimd.tensor_scalar(
                out=t_add[s][:],
                in0=nm_bc[g // 2][:, (g % 2) * 512 : (g % 2 + 1) * 512],
                scalar1=cols[:, ct : ct + 1],
                scalar2=cols[:, 4 + ct : 5 + ct],
                op0=ALU.mult,
                op1=ALU.add,
            )

        def noise_term_s(s):
            ct, g = s // NG, s % NG
            t_add[s] = keep.tile([P, 512], F32, name="t_add%d" % s)
            nc.scalar.activation(
                out=t_add[s][:],
                in_=nm_bc[g // 2][:, (g % 2) * 512 : (g % 2 + 1) * 512],
                func=ACT.Identity,
                bias=cols[:, 4 + ct : 5 + ct],
                scale=cols[:, ct : ct + 1],
            )

        w_grp = keep.tile([P, 512, 4], BF16, name="w_grp", align_bytes=64)
        w_codes = keep.tile([P, 512], U32, name="w_codes", align_bytes=64)
        w_scales = keep.tile([P, 512], U8, name="w_scales", align_bytes=64)

        def w_quant():
            nc.vector.tensor_copy(out=w_grp[:], in_=w_raw[:].rearrange("p t c -> p c t"))
            nc.vector.quantize_mx(
                out=w_codes[:].bitcast(FP8X4),
                scales=w_scales[:],
                in_=w_grp[:].rearrange("p c t -> p (c t)"),
            )

        x_grp = [keep.tile([P, 2048], BF16, name="x_grp%d" % g, align_bytes=64) for g in range(NG)]
        x_codes = [keep.tile([P, 512], U32, name="x_codes%d" % g, align_bytes=64) for g in range(NG)]
        x_scales = [keep.tile([P, 512], U8, name="x_scales%d" % g, align_bytes=64) for g in range(NG)]
        outv = out.rearrange("b h w c -> b (h w) c")
        acc_t = {}
        z_t = {}
        y_t = {}
        q_t = {}
        w_t = {}
        sum_t = {}
        st_t = {}
        sm = {}
        gb_sb = [keep.tile([P, 512], F32, name="gb_sb%d" % h) for h in range(2)]
        dlT = keep.tile([P, 4, P], BF16, name="dlT")

        def x_turn(g, tag):
            xw = x_sb[g][:].bitcast(F32)
            xgw = x_grp[g][:].bitcast(F32)
            for hh in range(2):
                xt = ps.tile([P, 4, P], F32, name="xt", tag=tag, bufs=2)
                for j in range(4):
                    col = (hh * 2 + j // 2) * 256 + (j % 2) * P
                    nc.tensor.transpose(xt[:, j, :], xw[:, col : col + P], ident_f[:])
                nc.scalar.copy(
                    out=xgw[:, hh * 512 : (hh + 1) * 512].rearrange(
                        "p (h b u) -> p h b u", h=2, u=2
                    ),
                    in_=xt[:].rearrange("p (h u) b -> p h b u", h=2),
                )

        def x_quant(g):
            nc.vector.quantize_mx(
                out=x_codes[g][:].bitcast(FP8X4), scales=x_scales[g][:], in_=x_grp[g][:]
            )

        def mx(s, times=1):
            ct, g = s // NG, s % NG
            acc = ps.tile([P, 512], F32, name="acc", tag="p", bufs=2)
            for rep in range(times):
                nc.tensor.matmul_mx(
                    out=acc[:],
                    lhsT=w_codes[:, ct * P : (ct + 1) * P].bitcast(FP8X4),
                    lhsT_scale=w_scales[:, ct * P : (ct + 1) * P],
                    rhs=x_codes[g][:].bitcast(FP8X4),
                    rhs_scale=x_scales[g][:],
                    start=True,
                    stop=True,
                )
            acc_t[s] = acc

        def z_only(s):
            z = work.tile([P, 512], F32, name="z", tag="z")
            nc.vector.tensor_tensor(out=z[:], in0=acc_t[s][:], in1=t_add[s][:], op=ALU.add)
            z_t[s] = z

        def y_only(s):
            z = z_t[s]
            yt = keep.tile([P, 512], F32, name="y%d" % s)
            nc.vector.scalar_tensor_tensor(
                out=yt[:], in0=z[:], scalar=SLOPE, in1=z[:], op0=ALU.mult, op1=ALU.max
            )
            y_t[s] = yt

        def square(s):
            qt = work.tile([P, 512], F32, name="qt", tag="q")
            nc.scalar.activation(out=qt[:], in_=y_t[s][:], func=ACT.Square)
            q_t[s] = qt

        def sums(s, k):
            ct, g = s // NG, s % NG
            if g == 0:
                acc_sum = ps.tile([P, P], F32, name="acc_sum", tag=("sy" if k == 0 else "sq"))
                sum_t[(ct, k)] = acc_sum
            if True:
                src = y_t[s] if k == 0 else q_t[s]
                for j in range(4):
                    hw = g * 4 + j
                    nc.tensor.matmul(
                        out=sum_t[(ct, k)][:],
                        lhsT=src[:, j * P : (j + 1) * P],
                        rhs=ident_f[:],
                        is_transpose=True,
                        start=(hw == 0),
                        stop=(hw == HW - 1),
                    )

        def stats_a(ct):
            mean = small.tile([P, P], F32, name="mean", tag="mean")
            nc.scalar.activation(out=mean[:], in_=sum_t[(ct, 0)][:], func=ACT.Copy, scale=1.0 / HW)
            msq = small.tile([P, P], F32, name="msq", tag="msq")
            nc.scalar.activation(out=msq[:], in_=sum_t[(ct, 0)][:], func=ACT.Square, scale=1.0 / HW)
            sm[("msq", ct)] = msq
            sm[("mean", ct)] = mean

        def stats_b(ct):
            var = small.tile([P, P], F32, name="var", tag="var")
            nc.vector.scalar_tensor_tensor(
                out=var[:], in0=sum_t[(ct, 1)][:], scalar=1.0 / HW, in1=sm[("msq", ct)][:],
                op0=ALU.mult, op1=ALU.subtract,
            )
            rstd = small.tile([P, P], F32, name="rstd", tag="rstd")
            nc.scalar.activation(
                out=rstd[:], in_=var[:], func=ACT.Abs_reciprocal_sqrt, bias=eps_t[:], scale=1.0
            )
            sm[("rstd", ct)] = rstd

        def stats_c(ct):
            cs = slice(ct * P, (ct + 1) * P)
            rstd = sm[("rstd", ct)]
            a_c = small.tile([P, P], F32, name="a_c", tag="a_c")
            nc.vector.tensor_tensor(out=a_c[:], in0=rstd[:], in1=gb_sb[0][:, cs], op=ALU.mult)
            sm[("ac", ct)] = a_c
            m_a = small.tile([P, P], F32, name="m_a", tag="m_a")
            nc.gpsimd.tensor_tensor(out=m_a[:], in0=sm[("mean", ct)][:], in1=a_c[:], op=ALU.mult)
            b_c = small.tile([P, P], F32, name="b_c", tag="b_c", bufs=3)
            nc.gpsimd.tensor_tensor(out=b_c[:], in0=gb_sb[1][:, cs], in1=m_a[:], op=ALU.subtract)
            sm[("b", ct)] = b_c

        def stats_d(ct):
            a_ps = ps.tile([P, P], F32, name="a_ps", tag="a", bufs=2)
            nc.tensor.transpose(a_ps[:], sm[("ac", ct)][:], ident_f[:])
            sm[("a", ct)] = a_ps

        def scale_y(e):
            ct = e // NG
            wt = work.tile([P, 4, P], F32, name="wt", tag="w", bufs=4)
            nc.vector.tensor_tensor(
                out=wt[:],
                in0=y_t[e][:].rearrange("p (h b) -> p h b", h=4),
                in1=sm[("a", ct)][:].unsqueeze(1).to_broadcast([P, 4, P]),
                op=ALU.mult,
            )
            w_t[e] = wt

        def turn_out(e, tag="o"):
            o_ps = ps.tile([P, 4, P], F32, name="o_ps", tag=tag, bufs=2)
            for j in range(4):
                nc.tensor.transpose(o_ps[:, j, :], w_t[e][:, j, :], ident_f[:])
            sm[("o", e)] = o_ps

        def shift_store(e):
            ct, g = e // NG, e % NG
            ot = work.tile([P, 4, P], F32, name="ot", tag="ot", bufs=8)
            nc.vector.tensor_tensor(
                out=ot[:],
                in0=sm[("o", e)][:],
                in1=sm[("b", ct)][:].unsqueeze(1).to_broadcast([P, 4, P]),
                op=ALU.add,
            )
            nc.sync.dma_start(out=outv[:, g * 4 : (g + 1) * 4, ct * P : (ct + 1) * P], in_=ot[:])

        def shift_store_sg(e):
            ct, g = e // NG, e % NG
            ev = work.tile([P, 4, P], F32, name="ev", tag="ev")
            nc.scalar.copy(out=ev[:], in_=sm[("o", e)][:])
            ot = work.tile([P, 4, P], F32, name="ot", tag="ot", bufs=8)
            nc.gpsimd.tensor_tensor(
                out=ot[:],
                in0=ev[:],
                in1=sm[("b", ct)][:].unsqueeze(1).to_broadcast([P, 4, P]),
                op=ALU.add,
            )
            nc.sync.dma_start(out=outv[:, g * 4 : (g + 1) * 4, ct * P : (ct + 1) * P], in_=ot[:])

        def shift(e):
            if e < 12 and e % 2 == 1 and USE_SG:
                shift_store_sg(e)
            else:
                shift_store(e)

        def style_turn():
            dlT_ps = ps.tile([P, 4, P], BF16, name="dlT_ps", tag="a", bufs=2)
            for kc in range(4):
                nc.tensor.transpose(dlT_ps[:, kc, :], dl_sb[:, kc * P : (kc + 1) * P], ident_b[:])
            nc.vector.tensor_copy(out=dlT[:], in_=dlT_ps[:])

        def style_mm(half):
            gb_ps = ps.tile([P, 512], F32, name="gb_ps", tag="o", bufs=2)
            for kc in range(4):
                nc.tensor.matmul(
                    out=gb_ps[:],
                    lhsT=dlT[:, kc, :],
                    rhs=dw_sb[:, kc, half * 512 : (half + 1) * 512],
                    start=(kc == 0),
                    stop=(kc == 3),
                )
            sm[("gb", half)] = gb_ps

        def style_out(half):
            nc.vector.scalar_tensor_tensor(
                out=gb_sb[half][:], in0=sm[("gb", half)][:], scalar=(1.0 if half == 0 else 0.0),
                in1=db_bc[:, half * 512 : (half + 1) * 512], op0=ALU.add, op1=ALU.add,
            )

        noise_half(0)
        x_turn(0, "o")
        noise_half(1)
        for s in range(NG):
            noise_term(s)
        w_quant()
        x_turn(1, "p")
        x_quant(0)
        x_turn(2, "o")
        mx(0)
        x_quant(1)
        x_turn(3, "o")
        mx(1)
        for i in range(NSTEP):
            rel = [(ct, i - (NG * ct + NG - 1)) for ct in range(NCT)]
            for ct, r in rel:
                if r == 2:
                    stats_a(ct)
            if i - LAG - 2 >= 0:
                shift(i - LAG - 2)
            if i == 6:
                style_out(0)
                style_out(1)
            for ct, r in rel:
                if r == 3:
                    stats_b(ct)
            for ct, r in rel:
                if r == 4:
                    stats_c(ct)
            if i - LAG - 1 >= 0:
                turn_out(i - LAG - 1)
            if i >= 2:
                sums(i - 2, 1)
            z_only(i)
            if i + 2 < NG:
                x_quant(i + 2)
            if i - LAG >= 0:
                scale_y(i - LAG)
            y_only(i)
            if i >= 1:
                sums(i - 1, 0)
            for ct, r in rel:
                if r == 4:
                    stats_d(ct)
            if i + 2 < NSTEP:
                mx(i + 2)
            if i + NG < NSTEP:
                noise_term_s(i + NG)
            square(i)
            if i == 3:
                style_turn()
            if i == 4:
                style_mm(0)
                style_mm(1)
        last = NCT - 1
        sums(NSTEP - 1, 0)
        sums(NSTEP - 2, 1)
        stats_a(last)
        shift(6)
        scale_y(8)
        turn_out(7, "o")
        sums(NSTEP - 1, 1)
        shift(7)
        scale_y(9)
        turn_out(8, "p")
        stats_b(last)
        shift(8)
        scale_y(10)
        turn_out(9, "p")
        shift(9)
        scale_y(11)
        turn_out(10, "o")
        stats_c(last)
        stats_d(last)
        shift(10)
        turn_out(11, "o")
        shift(11)
        for k in range(NG):
            scale_y(12 + k)
            turn_out(12 + k, "p" if k < 2 else "o")
        for k in range(NG):
            shift(12 + k)
